import numpy as np
import ml_dtypes


def mxq(x, axis, fmt="e4m3"):
    dtype, down = {"e4m3": (ml_dtypes.float8_e4m3fn, 7), "e5m2": (ml_dtypes.float8_e5m2, 14)}[fmt]
    v = np.moveaxis(np.asarray(x, np.float32).astype(ml_dtypes.bfloat16).astype(np.float64), axis, -1)
    blocks = v.reshape(v.shape[:-1] + (-1, 32))
    amax = np.abs(blocks).max(-1, keepdims=True)
    byte = np.maximum(np.where(amax > 0, np.frexp(amax)[1] - 1 + 127, 0) - down, 1)
    scale = np.exp2(byte - 127.0)
    codes = (blocks / scale).astype(np.float32).astype(dtype).astype(np.float64)
    return np.moveaxis((codes * scale).reshape(v.shape), -1, axis)


WIDE = False


def mx_kscale(k):
    if not WIDE:
        return np.ones(k)
    levels = np.array([20, -20, 10, -10, 0])
    a = np.random.permutation(np.resize(levels, k // 512 * 4)).reshape(k // 512, 4)
    idx = np.arange(k)
    return np.exp2(a[idx // 512, idx % 128 // 32])


BF16 = ml_dtypes.bfloat16


def bf(x):
    return np.asarray(x, np.float32).astype(BF16)


def f64(x):
    return np.asarray(x).astype(np.float64)


B, S, D_IN, D_OUT = 4, 2048, 512, 512


def setup_inputs():
    u = mx_kscale(D_OUT)
    x = np.random.standard_normal((B, S, D_IN))
    weight = np.random.standard_normal((D_OUT, D_IN)) * 0.04 / u[:, None]
    g = np.random.standard_normal((B, S, D_OUT)) * np.exp2(np.random.randint(-12, 1, (B, S, 1))) * 16.0 * u
    return {"x": bf(x), "weight": bf(weight), "grad_out": bf(g)}


def reference(x, weight, grad_out):
    g2 = f64(grad_out).reshape(-1, D_OUT)
    gq = mxq(g2, 1, "e5m2")
    wq = mxq(f64(weight), 0, "e4m3")
    gx = gq @ wq
    return gx.reshape(B, S, D_IN)

@@ -1,0 +1,131 @@
+from contextlib import ExitStack
+
+import concourse.mybir as mybir
+from concourse.masks import make_identity
+
+F32 = mybir.dt.float32
+BF16 = mybir.dt.bfloat16
+U32 = mybir.dt.uint32
+U8 = mybir.dt.uint8
+E4M3X4 = mybir.dt.float8_e4m3fn_x4
+E5M2X4 = mybir.dt.float8_e5m2_x4
+
+P = 128
+TOKENS = 8192
+K = 512
+N = 512
+SLOTS = TOKENS // P
+GROUP = 4
+GROUPS = SLOTS // GROUP
+LOAD_CUTS = [0, 4, 8, 16, 32, 48, 64]
+STORE_SLOTS = 8
+
+FLOPS = 2 * TOKENS * K * N
+BYTES = TOKENS * K * 2 + K * N * 2 + TOKENS * N * 4
+
+
+def tile_fp8purelinear_kernel(tc, x, weight, grad_out, out):
+    nc = tc.nc
+    g_view = grad_out.flatten_outer_dims().rearrange("(p s) k -> p (s k)", s=SLOTS)
+    o_view = out.flatten_outer_dims().rearrange("(p s) n -> p (s n)", s=SLOTS)
+
+    with ExitStack() as ctx:
+        keep = ctx.enter_context(tc.tile_pool(name="keep", bufs=1))
+        stage = ctx.enter_context(tc.tile_pool(name="stage", bufs=3))
+        xt_pool = ctx.enter_context(tc.psum_pool(name="xt_pool", bufs=2))
+        acc_pool = ctx.enter_context(tc.psum_pool(name="acc_pool", bufs=6))
+        ctx.enter_context(tc.manual_schedule())
+
+        w_raw = keep.tile([P, 4, N], BF16, name="w_raw")
+        nc.sync.dma_start(
+            out=w_raw[:].rearrange("p (u e) n -> p u e n", u=2),
+            in_=weight.rearrange("(u q e) n -> q u e n", u=2, e=2),
+        )
+        g_words = {}
+        for c in range(len(LOAD_CUTS) - 1):
+            s0, s1 = LOAD_CUTS[c], LOAD_CUTS[c + 1]
+            g_sb = keep.tile([P, (s1 - s0) * K], BF16, name="g_sb%d" % c)
+            nc.sync.dma_start(out=g_sb[:], in_=g_view[:, s0 * K : s1 * K])
+            words = g_sb[:].bitcast(F32)
+            for s in range(s0, s1):
+                g_words[s] = words[:, (s - s0) * (K // 2) : (s - s0 + 1) * (K // 2)]
+
+        ident = keep.tile([P, P], F32, name="ident")
+        make_identity(nc, ident[:])
+
+        w_grp = keep.tile([P, N, 4], BF16, name="w_grp", align_bytes=64)
+        nc.vector.tensor_copy(out=w_grp[:], in_=w_raw[:].rearrange("p t n -> p n t"))
+        w_codes = keep.tile([P, N], U32, name="w_codes", align_bytes=64)
+        w_scales = keep.tile([P, N], U8, name="w_scales", align_bytes=64)
+        nc.vector.quantize_mx(
+            out=w_codes[:].bitcast(E4M3X4),
+            scales=w_scales[:],
+            in_=w_grp[:].rearrange("p n t -> p (n t)"),
+        )
+
+        grouped = {}
+        codes = {}
+        scales = {}
+        o_tiles = {}
+
+        def transposes(g):
+            grp = stage.tile([P, GROUP * P * 4], BF16, name="grp", align_bytes=64)
+            grouped[g] = grp
+            grp_words = grp[:].bitcast(F32)
+            for h in range(2):
+                xt = xt_pool.tile([P, 2, 2, P], F32, name="xt")
+                for j in range(2):
+                    s = g * GROUP + 2 * h + j
+                    for u in range(2):
+                        nc.tensor.transpose(
+                            xt[:, j, u, :], g_words[s][:, u * P : (u + 1) * P], ident[:]
+                        )
+                nc.vector.tensor_copy(
+                    out=grp_words[:, h * 512 : (h + 1) * 512].rearrange(
+                        "p (j r u) -> p j r u", j=2, u=2
+                    ),
+                    in_=xt[:].rearrange("p j u r -> p j r u"),
+                )
+
+        def quantise(g):
+            cd = stage.tile([P, GROUP * P], U32, name="cd", align_bytes=64)
+            sc = stage.tile([P, GROUP * P], U8, name="sc", align_bytes=64)
+            codes[g] = cd
+            scales[g] = sc
+            nc.vector.quantize_mx(out=cd[:].bitcast(E5M2X4), scales=sc[:], in_=grouped[g][:])
+
+        def multiply(g):
+            for j in range(GROUP):
+                s = g * GROUP + j
+                chunk = s // STORE_SLOTS
+                if s % STORE_SLOTS == 0:
+                    o_tiles[chunk] = keep.tile([P, STORE_SLOTS * N], F32, name="o_sb%d" % chunk)
+                o_sb = o_tiles[chunk]
+                acc = acc_pool.tile([P, N], F32, name="acc")
+                cols = slice(j * P, (j + 1) * P)
+                nc.tensor.matmul_mx(
+                    out=acc[:],
+                    lhsT=codes[g][:, cols].bitcast(E5M2X4),
+                    lhsT_scale=scales[g][:, cols],
+                    rhs=w_codes[:].bitcast(E4M3X4),
+                    rhs_scale=w_scales[:],
+                    start=True,
+                    stop=True,
+                )
+                loc = s % STORE_SLOTS
+                nc.scalar.copy(out=o_sb[:, loc * N : (loc + 1) * N], in_=acc[:])
+                if loc == STORE_SLOTS - 1:
+                    nc.sync.dma_start(
+                        out=o_view[:, chunk * STORE_SLOTS * N : (chunk + 1) * STORE_SLOTS * N],
+                        in_=o_sb[:],
+                    )
+
+        transposes(0)
+        transposes(1)
+        quantise(0)
+        for g in range(GROUPS):
+            if g + 2 < GROUPS:
+                transposes(g + 2)
+            if g + 1 < GROUPS:
+                quantise(g + 1)
+            multiply(g)

@@ -17,8 +17,9 @@ N = 512
 SLOTS = TOKENS // P
 GROUP = 4
 GROUPS = SLOTS // GROUP
-LOAD_CUTS = [0, 4, 8, 16, 32, 48, 64]
-STORE_SLOTS = 8
+LOAD_CUTS = [0, 4, 8, 16, 32, 64]
+STORE_SLOTS = 16
+VECTOR_EVERY = 8
 
 FLOPS = 2 * TOKENS * K * N
 BYTES = TOKENS * K * 2 + K * N * 2 + TOKENS * N * 4
@@ -113,7 +114,10 @@ def tile_fp8purelinear_kernel(tc, x, weight, grad_out, out):
                     stop=True,
                 )
                 loc = s % STORE_SLOTS
-                nc.scalar.copy(out=o_sb[:, loc * N : (loc + 1) * N], in_=acc[:])
+                if s % VECTOR_EVERY == VECTOR_EVERY - 1:
+                    nc.vector.tensor_copy(out=o_sb[:, loc * N : (loc + 1) * N], in_=acc[:])
+                else:
+                    nc.scalar.copy(out=o_sb[:, loc * N : (loc + 1) * N], in_=acc[:])
                 if loc == STORE_SLOTS - 1:
                     nc.sync.dma_start(
                         out=o_view[:, chunk * STORE_SLOTS * N : (chunk + 1) * STORE_SLOTS * N],
@@ -121,9 +125,12 @@ def tile_fp8purelinear_kernel(tc, x, weight, grad_out, out):
                     )
 
         transposes(0)
-        transposes(1)
         quantise(0)
-        for g in range(GROUPS):
+        transposes(1)
+        multiply(0)
+        transposes(2)
+        quantise(1)
+        for g in range(1, GROUPS):
             if g + 2 < GROUPS:
                 transposes(g + 2)
             if g + 1 < GROUPS:

@@ -17,9 +17,9 @@ N = 512
 SLOTS = TOKENS // P
 GROUP = 4
 GROUPS = SLOTS // GROUP
-LOAD_CUTS = [0, 4, 8, 16, 32, 64]
-STORE_SLOTS = 16
-VECTOR_EVERY = 8
+LOAD_CUTS = [0, 4, 8, 16, 32, 48, 64]
+STORE_SLOTS = 8
+BLOCK = 16
 
 FLOPS = 2 * TOKENS * K * N
 BYTES = TOKENS * K * 2 + K * N * 2 + TOKENS * N * 4
@@ -27,8 +27,8 @@ BYTES = TOKENS * K * 2 + K * N * 2 + TOKENS * N * 4
 
 def tile_fp8purelinear_kernel(tc, x, weight, grad_out, out):
     nc = tc.nc
-    g_view = grad_out.flatten_outer_dims().rearrange("(p s) k -> p (s k)", s=SLOTS)
-    o_view = out.flatten_outer_dims().rearrange("(p s) n -> p (s n)", s=SLOTS)
+    g_view = grad_out.flatten_outer_dims().rearrange("(c p j) k -> c p (j k)", p=P, j=BLOCK)
+    o_view = out.flatten_outer_dims().rearrange("(c p j) n -> c p (j n)", p=P, j=BLOCK)
 
     with ExitStack() as ctx:
         keep = ctx.enter_context(tc.tile_pool(name="keep", bufs=1))
@@ -46,7 +46,10 @@ def tile_fp8purelinear_kernel(tc, x, weight, grad_out, out):
         for c in range(len(LOAD_CUTS) - 1):
             s0, s1 = LOAD_CUTS[c], LOAD_CUTS[c + 1]
             g_sb = keep.tile([P, (s1 - s0) * K], BF16, name="g_sb%d" % c)
-            nc.sync.dma_start(out=g_sb[:], in_=g_view[:, s0 * K : s1 * K])
+            j0 = s0 % BLOCK
+            nc.sync.dma_start(
+                out=g_sb[:], in_=g_view[s0 // BLOCK, :, j0 * K : (j0 + s1 - s0) * K]
+            )
             words = g_sb[:].bitcast(F32)
             for s in range(s0, s1):
                 g_words[s] = words[:, (s - s0) * (K // 2) : (s - s0 + 1) * (K // 2)]
@@ -114,23 +117,18 @@ def tile_fp8purelinear_kernel(tc, x, weight, grad_out, out):
                     stop=True,
                 )
                 loc = s % STORE_SLOTS
-                if s % VECTOR_EVERY == VECTOR_EVERY - 1:
-                    nc.vector.tensor_copy(out=o_sb[:, loc * N : (loc + 1) * N], in_=acc[:])
-                else:
-                    nc.scalar.copy(out=o_sb[:, loc * N : (loc + 1) * N], in_=acc[:])
+                nc.scalar.copy(out=o_sb[:, loc * N : (loc + 1) * N], in_=acc[:])
                 if loc == STORE_SLOTS - 1:
+                    j0 = (s + 1 - STORE_SLOTS) % BLOCK
                     nc.sync.dma_start(
-                        out=o_view[:, chunk * STORE_SLOTS * N : (chunk + 1) * STORE_SLOTS * N],
+                        out=o_view[s // BLOCK, :, j0 * N : (j0 + STORE_SLOTS) * N],
                         in_=o_sb[:],
                     )
 
         transposes(0)
-        quantise(0)
         transposes(1)
-        multiply(0)
-        transposes(2)
-        quantise(1)
-        for g in range(1, GROUPS):
+        quantise(0)
+        for g in range(GROUPS):
             if g + 2 < GROUPS:
                 transposes(g + 2)
             if g + 1 < GROUPS:

@@ -19,7 +19,6 @@ GROUP = 4
 GROUPS = SLOTS // GROUP
 LOAD_CUTS = [0, 4, 8, 16, 32, 48, 64]
 STORE_SLOTS = 8
-BLOCK = 16
 
 FLOPS = 2 * TOKENS * K * N
 BYTES = TOKENS * K * 2 + K * N * 2 + TOKENS * N * 4
@@ -27,8 +26,8 @@ BYTES = TOKENS * K * 2 + K * N * 2 + TOKENS * N * 4
 
 def tile_fp8purelinear_kernel(tc, x, weight, grad_out, out):
     nc = tc.nc
-    g_view = grad_out.flatten_outer_dims().rearrange("(c p j) k -> c p (j k)", p=P, j=BLOCK)
-    o_view = out.flatten_outer_dims().rearrange("(c p j) n -> c p (j n)", p=P, j=BLOCK)
+    g_view = grad_out.flatten_outer_dims().rearrange("(p s) k -> p (s k)", s=SLOTS)
+    o_view = out.flatten_outer_dims().rearrange("(p s) n -> p (s n)", s=SLOTS)
 
     with ExitStack() as ctx:
         keep = ctx.enter_context(tc.tile_pool(name="keep", bufs=1))
@@ -46,10 +45,7 @@ def tile_fp8purelinear_kernel(tc, x, weight, grad_out, out):
         for c in range(len(LOAD_CUTS) - 1):
             s0, s1 = LOAD_CUTS[c], LOAD_CUTS[c + 1]
             g_sb = keep.tile([P, (s1 - s0) * K], BF16, name="g_sb%d" % c)
-            j0 = s0 % BLOCK
-            nc.sync.dma_start(
-                out=g_sb[:], in_=g_view[s0 // BLOCK, :, j0 * K : (j0 + s1 - s0) * K]
-            )
+            nc.sync.dma_start(out=g_sb[:], in_=g_view[:, s0 * K : s1 * K])
             words = g_sb[:].bitcast(F32)
             for s in range(s0, s1):
                 g_words[s] = words[:, (s - s0) * (K // 2) : (s - s0 + 1) * (K // 2)]
@@ -119,9 +115,8 @@ def tile_fp8purelinear_kernel(tc, x, weight, grad_out, out):
                 loc = s % STORE_SLOTS
                 nc.scalar.copy(out=o_sb[:, loc * N : (loc + 1) * N], in_=acc[:])
                 if loc == STORE_SLOTS - 1:
-                    j0 = (s + 1 - STORE_SLOTS) % BLOCK
-                    nc.sync.dma_start(
-                        out=o_view[s // BLOCK, :, j0 * N : (j0 + STORE_SLOTS) * N],
+                    nc.scalar.dma_start(
+                        out=o_view[:, chunk * STORE_SLOTS * N : (chunk + 1) * STORE_SLOTS * N],
                         in_=o_sb[:],
                     )
 

from contextlib import ExitStack

import concourse.mybir as mybir
from concourse.masks import make_identity

F32 = mybir.dt.float32
BF16 = mybir.dt.bfloat16
U32 = mybir.dt.uint32
U8 = mybir.dt.uint8
E4M3X4 = mybir.dt.float8_e4m3fn_x4
E5M2X4 = mybir.dt.float8_e5m2_x4

P = 128
TOKENS = 8192
K = 512
N = 512
SLOTS = TOKENS // P
GROUP = 4
GROUPS = SLOTS // GROUP
LOAD_CUTS = [0, 4, 8, 16, 32, 48, 64]
STORE_SLOTS = 8

FLOPS = 2 * TOKENS * K * N
BYTES = TOKENS * K * 2 + K * N * 2 + TOKENS * N * 4


def tile_fp8purelinear_kernel(tc, x, weight, grad_out, out):
    nc = tc.nc
    g_view = grad_out.flatten_outer_dims().rearrange("(p s) k -> p (s k)", s=SLOTS)
    o_view = out.flatten_outer_dims().rearrange("(p s) n -> p (s n)", s=SLOTS)

    with ExitStack() as ctx:
        keep = ctx.enter_context(tc.tile_pool(name="keep", bufs=1))
        stage = ctx.enter_context(tc.tile_pool(name="stage", bufs=3))
        xt_pool = ctx.enter_context(tc.psum_pool(name="xt_pool", bufs=2))
        acc_pool = ctx.enter_context(tc.psum_pool(name="acc_pool", bufs=6))
        ctx.enter_context(tc.manual_schedule())

        w_raw = keep.tile([P, 4, N], BF16, name="w_raw")
        nc.sync.dma_start(
            out=w_raw[:].rearrange("p (u e) n -> p u e n", u=2),
            in_=weight.rearrange("(u q e) n -> q u e n", u=2, e=2),
        )
        g_words = {}
        for c in range(len(LOAD_CUTS) - 1):
            s0, s1 = LOAD_CUTS[c], LOAD_CUTS[c + 1]
            g_sb = keep.tile([P, (s1 - s0) * K], BF16, name="g_sb%d" % c)
            nc.sync.dma_start(out=g_sb[:], in_=g_view[:, s0 * K : s1 * K])
            words = g_sb[:].bitcast(F32)
            for s in range(s0, s1):
                g_words[s] = words[:, (s - s0) * (K // 2) : (s - s0 + 1) * (K // 2)]

        ident = keep.tile([P, P], F32, name="ident")
        make_identity(nc, ident[:])

        w_grp = keep.tile([P, N, 4], BF16, name="w_grp", align_bytes=64)
        nc.vector.tensor_copy(out=w_grp[:], in_=w_raw[:].rearrange("p t n -> p n t"))
        w_codes = keep.tile([P, N], U32, name="w_codes", align_bytes=64)
        w_scales = keep.tile([P, N], U8, name="w_scales", align_bytes=64)
        nc.vector.quantize_mx(
            out=w_codes[:].bitcast(E4M3X4),
            scales=w_scales[:],
            in_=w_grp[:].rearrange("p n t -> p (n t)"),
        )

        grouped = {}
        codes = {}
        scales = {}
        o_tiles = {}

        def transposes(g):
            grp = stage.tile([P, GROUP * P * 4], BF16, name="grp", align_bytes=64)
            grouped[g] = grp
            grp_words = grp[:].bitcast(F32)
            for h in range(2):
                xt = xt_pool.tile([P, 2, 2, P], F32, name="xt")
                for j in range(2):
                    s = g * GROUP + 2 * h + j
                    for u in range(2):
                        nc.tensor.transpose(
                            xt[:, j, u, :], g_words[s][:, u * P : (u + 1) * P], ident[:]
                        )
                nc.vector.tensor_copy(
                    out=grp_words[:, h * 512 : (h + 1) * 512].rearrange(
                        "p (j r u) -> p j r u", j=2, u=2
                    ),
                    in_=xt[:].rearrange("p j u r -> p j r u"),
                )

        def quantise(g):
            cd = stage.tile([P, GROUP * P], U32, name="cd", align_bytes=64)
            sc = stage.tile([P, GROUP * P], U8, name="sc", align_bytes=64)
            codes[g] = cd
            scales[g] = sc
            nc.vector.quantize_mx(out=cd[:].bitcast(E5M2X4), scales=sc[:], in_=grouped[g][:])

        def multiply(g):
            for j in range(GROUP):
                s = g * GROUP + j
                chunk = s // STORE_SLOTS
                if s % STORE_SLOTS == 0:
                    o_tiles[chunk] = keep.tile([P, STORE_SLOTS * N], F32, name="o_sb%d" % chunk)
                o_sb = o_tiles[chunk]
                acc = acc_pool.tile([P, N], F32, name="acc")
                cols = slice(j * P, (j + 1) * P)
                nc.tensor.matmul_mx(
                    out=acc[:],
                    lhsT=codes[g][:, cols].bitcast(E5M2X4),
                    lhsT_scale=scales[g][:, cols],
                    rhs=w_codes[:].bitcast(E4M3X4),
                    rhs_scale=w_scales[:],
                    start=True,
                    stop=True,
                )
                loc = s % STORE_SLOTS
                nc.scalar.copy(out=o_sb[:, loc * N : (loc + 1) * N], in_=acc[:])
                if loc == STORE_SLOTS - 1:
                    nc.scalar.dma_start(
                        out=o_view[:, chunk * STORE_SLOTS * N : (chunk + 1) * STORE_SLOTS * N],
                        in_=o_sb[:],
                    )

        transposes(0)
        transposes(1)
        quantise(0)
        for g in range(GROUPS):
            if g + 2 < GROUPS:
                transposes(g + 2)
            if g + 1 < GROUPS:
                quantise(g + 1)
            multiply(g)
